import numpy as np
import ml_dtypes

BF16 = ml_dtypes.bfloat16


def bf(x):
    return np.asarray(x, np.float32).astype(BF16)


def f32(x):
    return np.asarray(x, np.float32)


def f64(x):
    return np.asarray(x).astype(np.float64)


def striped(idx):
    return np.tile(idx.reshape(-1, 16).T, (8, 1))


C, H, S, N = 256, 128, 1024, 512
ANG_MAX = 1.5


def setup_inputs():
    return {"table": f32(np.random.standard_normal((C, S))), "pos": f32(np.random.standard_normal((C, N))), "ang": f32(np.random.uniform(-ANG_MAX, ANG_MAX, (H, N))), "offs": striped(np.random.permutation(np.tile(np.arange(S), 2))[:N])}


def reference(table, pos, ang, offs):
    idx = offs[:16].T.reshape(-1)
    e = f64(table)[:, idx] + f64(pos)
    a, b = e[:H], e[H:]
    co, si = np.cos(f64(ang)), np.sin(f64(ang))
    return np.concatenate([a * co - b * si, a * si + b * co], axis=0)

@@ -1,0 +1,59 @@
+import math
+
+import concourse.mybir as mybir
+
+F32 = mybir.dt.float32
+U16 = mybir.dt.uint16
+ADD = mybir.AluOpType.add
+SUBTRACT = mybir.AluOpType.subtract
+MULT = mybir.AluOpType.mult
+SIN = mybir.ActivationFunctionType.Sin
+
+P = 128
+VOCAB = 1024
+TOKENS = 512
+
+
+def tile_textdecoder_kernel(tc, table, pos, ang, offs, out):
+    nc = tc.nc
+    with tc.tile_pool(name="held", bufs=1) as held:
+        offsets = held.tile([P, TOKENS // 16], U16, name="offsets")
+        angle = held.tile([P, TOKENS], F32, name="angle")
+        table_a = held.tile([P, VOCAB], F32, name="table_a")
+        table_b = held.tile([P, VOCAB], F32, name="table_b")
+        pos_a = held.tile([P, TOKENS], F32, name="pos_a")
+        pos_b = held.tile([P, TOKENS], F32, name="pos_b")
+
+        nc.sync.dma_start(offsets[:], offs)
+        nc.scalar.dma_start(angle[:], ang)
+        nc.sync.dma_start(table_a[:], table[0:P, :])
+        nc.scalar.dma_start(pos_a[:], pos[0:P, :])
+        nc.sync.dma_start(table_b[:], table[P : 2 * P, :])
+        nc.scalar.dma_start(pos_b[:], pos[P : 2 * P, :])
+
+        half_pi = held.tile([P, 1], F32, name="half_pi")
+        nc.vector.memset(half_pi[:], math.pi / 2)
+        sin = held.tile([P, TOKENS], F32, name="sin")
+        cos = held.tile([P, TOKENS], F32, name="cos")
+        nc.scalar.activation(sin[:], angle[:], SIN)
+        nc.scalar.activation(cos[:], angle[:], SIN, bias=half_pi[:])
+
+        e_a = held.tile([P, TOKENS], F32, name="e_a")
+        a_cos = held.tile([P, TOKENS], F32, name="a_cos")
+        a_sin = held.tile([P, TOKENS], F32, name="a_sin")
+        nc.vector.tensor_tensor(e_a[:], table_a[:].indirect(offsets[:]), pos_a[:], ADD)
+        nc.vector.tensor_tensor(a_cos[:], e_a[:], cos[:], MULT)
+        nc.vector.tensor_tensor(a_sin[:], e_a[:], sin[:], MULT)
+
+        e_b = held.tile([P, TOKENS], F32, name="e_b")
+        b_sin = held.tile([P, TOKENS], F32, name="b_sin")
+        b_cos = held.tile([P, TOKENS], F32, name="b_cos")
+        out_a = held.tile([P, TOKENS], F32, name="out_a")
+        out_b = held.tile([P, TOKENS], F32, name="out_b")
+        nc.vector.tensor_tensor(e_b[:], table_b[:].indirect(offsets[:]), pos_b[:], ADD)
+        nc.vector.tensor_tensor(b_sin[:], e_b[:], sin[:], MULT)
+        nc.vector.tensor_tensor(out_a[:], a_cos[:], b_sin[:], SUBTRACT)
+        nc.sync.dma_start(out[0:P, :], out_a[:])
+        nc.vector.tensor_tensor(b_cos[:], e_b[:], cos[:], MULT)
+        nc.vector.tensor_tensor(out_b[:], a_sin[:], b_cos[:], ADD)
+        nc.scalar.dma_start(out[P : 2 * P, :], out_b[:])

@@ -12,6 +12,7 @@ SIN = mybir.ActivationFunctionType.Sin
 P = 128
 VOCAB = 1024
 TOKENS = 512
+HALF = TOKENS // 2
 
 
 def tile_textdecoder_kernel(tc, table, pos, ang, offs, out):
@@ -25,9 +26,9 @@ def tile_textdecoder_kernel(tc, table, pos, ang, offs, out):
         pos_b = held.tile([P, TOKENS], F32, name="pos_b")
 
         nc.sync.dma_start(offsets[:], offs)
-        nc.scalar.dma_start(angle[:], ang)
-        nc.sync.dma_start(table_a[:], table[0:P, :])
         nc.scalar.dma_start(pos_a[:], pos[0:P, :])
+        nc.sync.dma_start(table_a[:], table[0:P, :])
+        nc.scalar.dma_start(angle[:], ang)
         nc.sync.dma_start(table_b[:], table[P : 2 * P, :])
         nc.scalar.dma_start(pos_b[:], pos[P : 2 * P, :])
 
@@ -38,22 +39,25 @@ def tile_textdecoder_kernel(tc, table, pos, ang, offs, out):
         nc.scalar.activation(sin[:], angle[:], SIN)
         nc.scalar.activation(cos[:], angle[:], SIN, bias=half_pi[:])
 
-        e_a = held.tile([P, TOKENS], F32, name="e_a")
-        a_cos = held.tile([P, TOKENS], F32, name="a_cos")
+        pieces = [slice(0, HALF), slice(HALF, TOKENS)]
+        lists = [offsets[:, 0 : HALF // 16], offsets[:, HALF // 16 : TOKENS // 16]]
         a_sin = held.tile([P, TOKENS], F32, name="a_sin")
-        nc.vector.tensor_tensor(e_a[:], table_a[:].indirect(offsets[:]), pos_a[:], ADD)
-        nc.vector.tensor_tensor(a_cos[:], e_a[:], cos[:], MULT)
-        nc.vector.tensor_tensor(a_sin[:], e_a[:], sin[:], MULT)
-
-        e_b = held.tile([P, TOKENS], F32, name="e_b")
+        a_cos = held.tile([P, TOKENS], F32, name="a_cos")
         b_sin = held.tile([P, TOKENS], F32, name="b_sin")
         b_cos = held.tile([P, TOKENS], F32, name="b_cos")
         out_a = held.tile([P, TOKENS], F32, name="out_a")
         out_b = held.tile([P, TOKENS], F32, name="out_b")
-        nc.vector.tensor_tensor(e_b[:], table_b[:].indirect(offsets[:]), pos_b[:], ADD)
-        nc.vector.tensor_tensor(b_sin[:], e_b[:], sin[:], MULT)
+        for table_half, pos_half, e_sin, e_cos in (
+            (table_a, pos_a, a_sin, a_cos),
+            (table_b, pos_b, b_sin, b_cos),
+        ):
+            e = [held.tile([P, HALF], F32, name=f"e_{k}") for k in range(2)]
+            for k in range(2):
+                nc.vector.tensor_tensor(e[k][:], table_half[:].indirect(lists[k]), pos_half[:, pieces[k]], ADD)
+            for k in range(2):
+                nc.vector.tensor_tensor(e_sin[:, pieces[k]], e[k][:], sin[:, pieces[k]], MULT)
+                nc.vector.tensor_tensor(e_cos[:, pieces[k]], e[k][:], cos[:, pieces[k]], MULT)
         nc.vector.tensor_tensor(out_a[:], a_cos[:], b_sin[:], SUBTRACT)
         nc.sync.dma_start(out[0:P, :], out_a[:])
-        nc.vector.tensor_tensor(b_cos[:], e_b[:], cos[:], MULT)
         nc.vector.tensor_tensor(out_b[:], a_sin[:], b_cos[:], ADD)
         nc.scalar.dma_start(out[P : 2 * P, :], out_b[:])

@@ -28,9 +28,9 @@ def tile_textdecoder_kernel(tc, table, pos, ang, offs, out):
         nc.sync.dma_start(offsets[:], offs)
         nc.scalar.dma_start(pos_a[:], pos[0:P, :])
         nc.sync.dma_start(table_a[:], table[0:P, :])
-        nc.scalar.dma_start(angle[:], ang)
+        nc.sync.dma_start(angle[:], ang)
         nc.sync.dma_start(table_b[:], table[P : 2 * P, :])
-        nc.scalar.dma_start(pos_b[:], pos[P : 2 * P, :])
+        nc.sync.dma_start(pos_b[:], pos[P : 2 * P, :])
 
         half_pi = held.tile([P, 1], F32, name="half_pi")
         nc.vector.memset(half_pi[:], math.pi / 2)

@@ -25,9 +25,9 @@ def tile_textdecoder_kernel(tc, table, pos, ang, offs, out):
         pos_a = held.tile([P, TOKENS], F32, name="pos_a")
         pos_b = held.tile([P, TOKENS], F32, name="pos_b")
 
-        nc.sync.dma_start(offsets[:], offs)
-        nc.scalar.dma_start(pos_a[:], pos[0:P, :])
         nc.sync.dma_start(table_a[:], table[0:P, :])
+        nc.scalar.dma_start(pos_a[:], pos[0:P, :])
+        nc.sync.dma_start(offsets[:], offs)
         nc.sync.dma_start(angle[:], ang)
         nc.sync.dma_start(table_b[:], table[P : 2 * P, :])
         nc.sync.dma_start(pos_b[:], pos[P : 2 * P, :])

@@ -12,7 +12,7 @@ SIN = mybir.ActivationFunctionType.Sin
 P = 128
 VOCAB = 1024
 TOKENS = 512
-HALF = TOKENS // 2
+CUT = 3 * TOKENS // 4
 
 
 def tile_textdecoder_kernel(tc, table, pos, ang, offs, out):
@@ -39,25 +39,35 @@ def tile_textdecoder_kernel(tc, table, pos, ang, offs, out):
         nc.scalar.activation(sin[:], angle[:], SIN)
         nc.scalar.activation(cos[:], angle[:], SIN, bias=half_pi[:])
 
-        pieces = [slice(0, HALF), slice(HALF, TOKENS)]
-        lists = [offsets[:, 0 : HALF // 16], offsets[:, HALF // 16 : TOKENS // 16]]
+        pieces = [slice(0, CUT), slice(CUT, TOKENS)]
+        lists = [offsets[:, 0 : CUT // 16], offsets[:, CUT // 16 : TOKENS // 16]]
+        e_a = [
+            held.tile([P, CUT], F32, name="e_a_long"),
+            held.tile([P, TOKENS - CUT], F32, name="e_a_short", tag="e_a_short_then_e_b"),
+        ]
         a_sin = held.tile([P, TOKENS], F32, name="a_sin")
         a_cos = held.tile([P, TOKENS], F32, name="a_cos")
+        for k in (0, 1):
+            nc.vector.tensor_tensor(e_a[k][:], table_a[:].indirect(lists[k]), pos_a[:, pieces[k]], ADD)
+        for k in (0, 1):
+            nc.vector.tensor_tensor(a_sin[:, pieces[k]], e_a[k][:], sin[:, pieces[k]], MULT)
+        for k in (1, 0):
+            nc.vector.tensor_tensor(a_cos[:, pieces[k]], e_a[k][:], cos[:, pieces[k]], MULT)
+
+        e_b = held.tile([P, TOKENS], F32, name="e_b", tag="e_a_short_then_e_b")
         b_sin = held.tile([P, TOKENS], F32, name="b_sin")
         b_cos = held.tile([P, TOKENS], F32, name="b_cos")
         out_a = held.tile([P, TOKENS], F32, name="out_a")
         out_b = held.tile([P, TOKENS], F32, name="out_b")
-        for table_half, pos_half, e_sin, e_cos in (
-            (table_a, pos_a, a_sin, a_cos),
-            (table_b, pos_b, b_sin, b_cos),
-        ):
-            e = [held.tile([P, HALF], F32, name=f"e_{k}") for k in range(2)]
-            for k in range(2):
-                nc.vector.tensor_tensor(e[k][:], table_half[:].indirect(lists[k]), pos_half[:, pieces[k]], ADD)
-            for k in range(2):
-                nc.vector.tensor_tensor(e_sin[:, pieces[k]], e[k][:], sin[:, pieces[k]], MULT)
-                nc.vector.tensor_tensor(e_cos[:, pieces[k]], e[k][:], cos[:, pieces[k]], MULT)
+        for piece, entries in zip(pieces, lists):
+            nc.vector.tensor_tensor(e_b[:, piece], table_b[:].indirect(entries), pos_b[:, piece], ADD)
+        for piece in pieces:
+            nc.vector.tensor_tensor(b_sin[:, piece], e_b[:, piece], sin[:, piece], MULT)
+        long, short = pieces
+        nc.vector.tensor_tensor(b_cos[:, long], e_b[:, long], cos[:, long], MULT)
         nc.vector.tensor_tensor(out_a[:], a_cos[:], b_sin[:], SUBTRACT)
         nc.sync.dma_start(out[0:P, :], out_a[:])
-        nc.vector.tensor_tensor(out_b[:], a_sin[:], b_cos[:], ADD)
+        nc.vector.tensor_tensor(b_cos[:, short], e_b[:, short], cos[:, short], MULT)
+        for piece in pieces:
+            nc.vector.tensor_tensor(out_b[:, piece], a_sin[:, piece], b_cos[:, piece], ADD)
         nc.scalar.dma_start(out[P : 2 * P, :], out_b[:])

@@ -32,15 +32,17 @@ def tile_textdecoder_kernel(tc, table, pos, ang, offs, out):
         nc.sync.dma_start(table_b[:], table[P : 2 * P, :])
         nc.sync.dma_start(pos_b[:], pos[P : 2 * P, :])
 
+        pieces = [slice(0, CUT), slice(CUT, TOKENS)]
+        lists = [offsets[:, 0 : CUT // 16], offsets[:, CUT // 16 : TOKENS // 16]]
         half_pi = held.tile([P, 1], F32, name="half_pi")
         nc.vector.memset(half_pi[:], math.pi / 2)
         sin = held.tile([P, TOKENS], F32, name="sin")
         cos = held.tile([P, TOKENS], F32, name="cos")
-        nc.scalar.activation(sin[:], angle[:], SIN)
-        nc.scalar.activation(cos[:], angle[:], SIN, bias=half_pi[:])
+        for k in (0, 1):
+            nc.scalar.activation(sin[:, pieces[k]], angle[:, pieces[k]], SIN)
+        for k in (1, 0):
+            nc.scalar.activation(cos[:, pieces[k]], angle[:, pieces[k]], SIN, bias=half_pi[:])
 
-        pieces = [slice(0, CUT), slice(CUT, TOKENS)]
-        lists = [offsets[:, 0 : CUT // 16], offsets[:, CUT // 16 : TOKENS // 16]]
         e_a = [
             held.tile([P, CUT], F32, name="e_a_long"),
             held.tile([P, TOKENS - CUT], F32, name="e_a_short", tag="e_a_short_then_e_b"),

import math

import concourse.mybir as mybir

F32 = mybir.dt.float32
U16 = mybir.dt.uint16
ADD = mybir.AluOpType.add
SUBTRACT = mybir.AluOpType.subtract
MULT = mybir.AluOpType.mult
SIN = mybir.ActivationFunctionType.Sin

P = 128
VOCAB = 1024
TOKENS = 512
CUT = 3 * TOKENS // 4


def tile_textdecoder_kernel(tc, table, pos, ang, offs, out):
    nc = tc.nc
    with tc.tile_pool(name="held", bufs=1) as held:
        offsets = held.tile([P, TOKENS // 16], U16, name="offsets")
        angle = held.tile([P, TOKENS], F32, name="angle")
        table_a = held.tile([P, VOCAB], F32, name="table_a")
        table_b = held.tile([P, VOCAB], F32, name="table_b")
        pos_a = held.tile([P, TOKENS], F32, name="pos_a")
        pos_b = held.tile([P, TOKENS], F32, name="pos_b")

        nc.sync.dma_start(table_a[:], table[0:P, :])
        nc.scalar.dma_start(pos_a[:], pos[0:P, :])
        nc.sync.dma_start(offsets[:], offs)
        nc.sync.dma_start(angle[:], ang)
        nc.sync.dma_start(table_b[:], table[P : 2 * P, :])
        nc.sync.dma_start(pos_b[:], pos[P : 2 * P, :])

        pieces = [slice(0, CUT), slice(CUT, TOKENS)]
        lists = [offsets[:, 0 : CUT // 16], offsets[:, CUT // 16 : TOKENS // 16]]
        half_pi = held.tile([P, 1], F32, name="half_pi")
        nc.vector.memset(half_pi[:], math.pi / 2)
        sin = held.tile([P, TOKENS], F32, name="sin")
        cos = held.tile([P, TOKENS], F32, name="cos")
        for k in (0, 1):
            nc.scalar.activation(sin[:, pieces[k]], angle[:, pieces[k]], SIN)
        for k in (1, 0):
            nc.scalar.activation(cos[:, pieces[k]], angle[:, pieces[k]], SIN, bias=half_pi[:])

        e_a = [
            held.tile([P, CUT], F32, name="e_a_long"),
            held.tile([P, TOKENS - CUT], F32, name="e_a_short", tag="e_a_short_then_e_b"),
        ]
        a_sin = held.tile([P, TOKENS], F32, name="a_sin")
        a_cos = held.tile([P, TOKENS], F32, name="a_cos")
        for k in (0, 1):
            nc.vector.tensor_tensor(e_a[k][:], table_a[:].indirect(lists[k]), pos_a[:, pieces[k]], ADD)
        for k in (0, 1):
            nc.vector.tensor_tensor(a_sin[:, pieces[k]], e_a[k][:], sin[:, pieces[k]], MULT)
        for k in (1, 0):
            nc.vector.tensor_tensor(a_cos[:, pieces[k]], e_a[k][:], cos[:, pieces[k]], MULT)

        e_b = held.tile([P, TOKENS], F32, name="e_b", tag="e_a_short_then_e_b")
        b_sin = held.tile([P, TOKENS], F32, name="b_sin")
        b_cos = held.tile([P, TOKENS], F32, name="b_cos")
        out_a = held.tile([P, TOKENS], F32, name="out_a")
        out_b = held.tile([P, TOKENS], F32, name="out_b")
        for piece, entries in zip(pieces, lists):
            nc.vector.tensor_tensor(e_b[:, piece], table_b[:].indirect(entries), pos_b[:, piece], ADD)
        for piece in pieces:
            nc.vector.tensor_tensor(b_sin[:, piece], e_b[:, piece], sin[:, piece], MULT)
        long, short = pieces
        nc.vector.tensor_tensor(b_cos[:, long], e_b[:, long], cos[:, long], MULT)
        nc.vector.tensor_tensor(out_a[:], a_cos[:], b_sin[:], SUBTRACT)
        nc.sync.dma_start(out[0:P, :], out_a[:])
        nc.vector.tensor_tensor(b_cos[:, short], e_b[:, short], cos[:, short], MULT)
        for piece in pieces:
            nc.vector.tensor_tensor(out_b[:, piece], a_sin[:, piece], b_cos[:, piece], ADD)
        nc.scalar.dma_start(out[P : 2 * P, :], out_b[:])
